import numpy as np
import ml_dtypes


def mxq(x, axis, fmt="e4m3"):
    dtype, down = {"e4m3": (ml_dtypes.float8_e4m3fn, 7), "e5m2": (ml_dtypes.float8_e5m2, 14)}[fmt]
    v = np.moveaxis(np.asarray(x, np.float32).astype(ml_dtypes.bfloat16).astype(np.float64), axis, -1)
    blocks = v.reshape(v.shape[:-1] + (-1, 32))
    amax = np.abs(blocks).max(-1, keepdims=True)
    byte = np.maximum(np.where(amax > 0, np.frexp(amax)[1] - 1 + 127, 0) - down, 1)
    scale = np.exp2(byte - 127.0)
    codes = (blocks / scale).astype(np.float32).astype(dtype).astype(np.float64)
    return np.moveaxis((codes * scale).reshape(v.shape), -1, axis)


WIDE = False


def mx_kscale(k):
    if not WIDE:
        return np.ones(k)
    levels = np.array([10, -10, 5, -5, 0])
    a = np.random.permutation(np.resize(levels, k // 512 * 4)).reshape(k // 512, 4)
    idx = np.arange(k)
    return np.exp2(a[idx // 512, idx % 128 // 32])


BF16 = ml_dtypes.bfloat16


def bf(x):
    return np.asarray(x, np.float32).astype(BF16)


def f64(x):
    return np.asarray(x).astype(np.float64)


B, S, IN, OUT, SPLIT = 4, 1024, 1024, 256, 512


def binarise(w):
    return np.sign(w)


def branch(x2d, V, U, v2, v1, u2, u1):
    v1u2 = v1 * u2
    h = mxq(x2d * v2, 1, "e4m3") @ mxq(binarise(V), 1, "e4m3").T
    return (mxq(h * v1u2, 1, "e4m3") @ mxq(binarise(U), 1, "e4m3").T) * u1


def setup_inputs():
    n = np.random.standard_normal
    s, t = mx_kscale(IN), mx_kscale(SPLIT)
    rs = s[np.arange(SPLIT) * IN // SPLIT]
    rt = t[np.arange(OUT) * SPLIT // OUT]
    mv = np.where(rs[:, None] == s[None, :], 1.0, 0.0)
    mu = np.where(rt[:, None] == t[None, :], 1.0, 0.0)
    gv = np.sqrt(IN / mv.sum(1))
    gu = np.sqrt(SPLIT / mu.sum(1))
    return {
        "x": bf(n((B, S, IN))),
        "V": bf(n((SPLIT, IN)) * mv),
        "U": bf(n((OUT, SPLIT)) * mu),
        "v2": bf(n((1, IN)) * 5.0 / np.sqrt(IN) * s),
        "v1": bf(n((1, SPLIT)) * 0.3 * gv / rs),
        "u2": bf(n((1, SPLIT)) * 0.3 * t),
        "u1": bf(n((1, OUT)) * 3.0 / np.sqrt(SPLIT) * gu / rt),
        "V_R": bf(n((SPLIT, IN)) * mv),
        "U_R": bf(n((OUT, SPLIT)) * mu),
        "v2_R": bf(n((1, IN)) * 5.0 / np.sqrt(IN) * s),
        "v1_R": bf(n((1, SPLIT)) * 0.3 * gv / rs),
        "u2_R": bf(n((1, SPLIT)) * 0.3 * t),
        "u1_R": bf(n((1, OUT)) * 3.0 / np.sqrt(SPLIT) * gu / rt),
        "bias": bf(n(OUT) * 0.3),
    }


def reference(x, V, U, v2, v1, u2, u1, V_R, U_R, v2_R, v1_R, u2_R, u1_R, bias):
    x = f64(x)
    lead = x.shape[:-1]
    x2d = x.reshape(-1, x.shape[-1])
    y = branch(x2d, f64(V), f64(U), f64(v2), f64(v1), f64(u2), f64(u1))
    y = y + branch(x2d, f64(V_R), f64(U_R), f64(v2_R), f64(v1_R), f64(u2_R), f64(u1_R))
    y = y + f64(bias)
    return y.reshape(lead + (U.shape[0],))

@@ -1,0 +1,357 @@
+from contextlib import ExitStack
+
+import concourse.mybir as mybir
+from concourse.masks import make_identity
+
+F32 = mybir.dt.float32
+BF16 = mybir.dt.bfloat16
+U32 = mybir.dt.uint32
+U8 = mybir.dt.uint8
+FP8X4 = mybir.dt.float8_e4m3fn_x4
+ACT = mybir.ActivationFunctionType
+ALU = mybir.AluOpType
+
+P = 128
+PACK = 4
+PAIR = 2
+K_PASS = P * PACK
+
+ROWS = 4096
+IN_F = 1024
+HID_F = 512
+OUT_F = 256
+BRANCHES = 2
+
+CHUNK = 512
+N_CHUNKS = ROWS // CHUNK
+ROW_TILES = CHUNK // P
+X_PASSES = IN_F // K_PASS
+HID_TILES = HID_F // P
+OUT_TILES = OUT_F // P
+HALF = 256
+assert HID_F == K_PASS and HID_TILES == PACK
+
+V1_COL = (0, 8)
+U1_COL = (16, 18)
+BIAS_COL = 20
+N_COLUMNS = 22
+
+FLOPS = BRANCHES * 2 * ROWS * (IN_F * HID_F + HID_F * OUT_F)
+
+
+def tile_littlebititqspeclinear_pa_t_kernel(
+    tc, x, V, U, v2, v1, u2, u1, V_R, U_R, v2_R, v1_R, u2_R, u1_R, bias, out
+):
+    nc = tc.nc
+    x_rows = x.flatten_outer_dims()
+    out_rows = out.flatten_outer_dims()
+
+    with ExitStack() as pools:
+        const = pools.enter_context(tc.tile_pool(name="const", bufs=1))
+        weight_stage = pools.enter_context(tc.tile_pool(name="weight_stage", bufs=2))
+        x_pool = pools.enter_context(tc.tile_pool(name="x_pool", bufs=N_CHUNKS))
+        one_chunk = pools.enter_context(tc.tile_pool(name="one_chunk", bufs=BRANCHES))
+        two_chunks = pools.enter_context(tc.tile_pool(name="two_chunks", bufs=2 * BRANCHES))
+        out_pool = pools.enter_context(tc.tile_pool(name="out_pool", bufs=2))
+        x_psum = pools.enter_context(tc.psum_pool(name="x_psum", bufs=4))
+        psum = pools.enter_context(tc.psum_pool(name="psum", bufs=4))
+
+        x_in = {}
+
+        def load_x(c):
+            x_tile = x_pool.tile([P, ROW_TILES, IN_F], BF16)
+            source = x_rows[c * CHUNK : (c + 1) * CHUNK, :].rearrange("(p i) k -> p i k", i=ROW_TILES)
+            for half in range(2):
+                tiles = slice(half * 2, half * 2 + 2)
+                nc.sync.dma_start(out=x_tile[:, tiles, :], in_=source[:, tiles, :])
+            x_in[c] = x_tile
+
+        v2_rows = const.tile([P, PAIR * P], BF16)
+        nc.vector.memset(v2_rows[:], 0.0)
+        for b, vector in enumerate((v2, v2_R)):
+            nc.scalar.dma_start(
+                out=v2_rows[4 * b : 4 * b + 4, :], in_=vector.rearrange("o (f w) -> (o f) w", w=PAIR * P)
+            )
+        load_x(0)
+
+        v_in = []
+        for weight in (V, V_R):
+            v_tile = weight_stage.tile([P, HID_TILES, IN_F], BF16)
+            nc.sync.dma_start(out=v_tile[:], in_=weight.rearrange("(m p) k -> p m k", p=P))
+            v_in.append(v_tile)
+
+        vector_rows = const.tile([P, P], BF16)
+        nc.vector.memset(vector_rows[:], 0.0)
+        first_row = 0
+        for vector in (v1, u2, v1_R, u2_R, u1, u1_R):
+            n_rows = vector.shape[1] // P
+            nc.scalar.dma_start(
+                out=vector_rows[first_row : first_row + n_rows, :], in_=vector.rearrange("o (j p) -> (o j) p", p=P)
+            )
+            first_row += n_rows
+        nc.scalar.dma_start(
+            out=vector_rows[BIAS_COL : BIAS_COL + OUT_TILES, :], in_=bias.rearrange("(j p) -> j p", p=P)
+        )
+
+        u_in = []
+        for weight in (U, U_R):
+            u_tile = weight_stage.tile([P, OUT_TILES, HID_F], BF16)
+            nc.scalar.dma_start(out=u_tile[:], in_=weight.rearrange("(j p) s -> p j s", p=P))
+            u_in.append(u_tile)
+
+        for c in range(1, N_CHUNKS):
+            load_x(c)
+
+        ident_f32 = const.tile([P, P], F32)
+        make_identity(nc, ident_f32[:])
+        ident_bf16 = const.tile([P, P], BF16)
+        make_identity(nc, ident_bf16[:])
+
+        def in_range(c):
+            return 0 <= c < N_CHUNKS
+
+        v2_bank = psum.tile([P, P], F32, tag="bank")
+        nc.tensor.transpose(v2_bank[:], v2_rows[:].bitcast(F32), ident_f32[:])
+        v2_words = const.tile([P, BRANCHES * X_PASSES * 2], F32)
+        nc.vector.tensor_copy(out=v2_words[:], in_=v2_bank[:, 0 : BRANCHES * X_PASSES * 2])
+        v2_values = v2_words[:].bitcast(BF16).rearrange("p (b g t) -> p b g t", b=BRANCHES, g=X_PASSES)
+
+        x_banks = {}
+
+        def transpose_x(c):
+            if not in_range(c):
+                return
+            x_words = x_in[c][:].bitcast(F32)
+            x_banks[c] = []
+            for half in range(2):
+                for g in range(X_PASSES):
+                    x_bank = x_psum.tile([P, 2, HALF], F32)
+                    for u in range(2):
+                        words = slice((2 * g + u) * P, (2 * g + u + 1) * P)
+                        for i in range(2):
+                            nc.tensor.transpose(
+                                x_bank[:, u, i * P : (i + 1) * P], x_words[:, 2 * half + i, words], ident_f32[:]
+                            )
+                    x_banks[c].append((half, g, x_bank))
+
+        x_scaled = {}
+
+        def scale_x(c):
+            if not in_range(c):
+                return
+            for b in range(BRANCHES):
+                scaled = one_chunk.tile([P, X_PASSES, CHUNK, PACK], BF16, align_bytes=64)
+                x_scaled[(c, b)] = scaled
+            for half, g, x_bank in x_banks[c]:
+                columns_of_half = slice(half * HALF, (half + 1) * HALF)
+                for b in range(BRANCHES):
+                    nc.vector.tensor_tensor(
+                        out=x_scaled[(c, b)][:, g, columns_of_half, :].rearrange("p c (u e) -> p c u e", e=PAIR),
+                        in0=x_bank[:].bitcast(BF16).rearrange("p u (c e) -> p c u e", e=PAIR),
+                        in1=v2_values[:, b, g, :]
+                        .rearrange("p (u e) -> p u e", e=PAIR)
+                        .unsqueeze(1)
+                        .to_broadcast([P, HALF, 2, PAIR]),
+                        op=ALU.mult,
+                    )
+
+        x_mx = {}
+
+        def quantise_x(c, b):
+            if not in_range(c):
+                return
+            x_codes = two_chunks.tile([P, X_PASSES, CHUNK], U32, align_bytes=64)
+            x_scales = two_chunks.tile([P, X_PASSES, CHUNK], U8, align_bytes=64)
+            nc.vector.quantize_mx(
+                out=x_codes[:].rearrange("p g c -> p (g c)").bitcast(FP8X4),
+                scales=x_scales[:].rearrange("p g c -> p (g c)"),
+                in_=x_scaled[(c, b)][:].rearrange("p g c t -> p (g c t)"),
+            )
+            x_mx[(c, b)] = (x_codes, x_scales)
+
+        v_mx = []
+        u_mx = []
+        h_planes = {}
+
+        def first_product(c):
+            if not in_range(c):
+                return
+            for b in range(BRANCHES):
+                v_codes, v_scales = v_mx[b]
+                x_codes, x_scales = x_mx[(c, b)]
+                h_plane = two_chunks.tile([P, HID_TILES, CHUNK], BF16)
+                for t in range(HID_TILES):
+                    features = slice(t * P, (t + 1) * P)
+                    h_bank = psum.tile([P, CHUNK], F32, tag="bank")
+                    for g in range(X_PASSES):
+                        nc.tensor.matmul_mx(
+                            out=h_bank[:],
+                            lhsT=v_codes[:, g, features].bitcast(FP8X4),
+                            lhsT_scale=v_scales[:, g, features],
+                            rhs=x_codes[:, g, :].bitcast(FP8X4),
+                            rhs_scale=x_scales[:, g, :],
+                            start=(g == 0),
+                            stop=(g == X_PASSES - 1),
+                        )
+                    nc.scalar.activation(
+                        out=h_plane[:, t, :], in_=h_bank[:], func=ACT.Copy, scale=hidden_scale[:, b, t : t + 1]
+                    )
+                h_planes[(c, b)] = h_plane
+
+        h_grouped = {}
+
+        def group_h(c, b):
+            if not in_range(c):
+                return
+            grouped = one_chunk.tile([P, CHUNK, PACK], BF16, align_bytes=64)
+            nc.vector.tensor_copy(
+                out=grouped[:].rearrange("p (c i) t -> p c t i", i=4),
+                in_=h_planes[(c, b)][:].rearrange("p t (c i) -> p c t i", i=4),
+            )
+            h_grouped[(c, b)] = grouped
+
+        h_mx = {}
+
+        def quantise_h(c, b):
+            if not in_range(c):
+                return
+            h_codes = two_chunks.tile([P, CHUNK], U32, align_bytes=64)
+            h_scales = two_chunks.tile([P, CHUNK], U8, align_bytes=64)
+            nc.vector.quantize_mx(
+                out=h_codes[:].bitcast(FP8X4),
+                scales=h_scales[:],
+                in_=h_grouped[(c, b)][:].rearrange("p c t -> p (c t)"),
+            )
+            h_mx[(c, b)] = (h_codes, h_scales)
+
+        y_scaled = {}
+
+        def second_product(c):
+            if not in_range(c):
+                return
+            for b in range(BRANCHES):
+                u_codes, u_scales = u_mx[b]
+                h_codes, h_scales = h_mx[(c, b)]
+                y_t = two_chunks.tile([P, OUT_TILES, CHUNK], F32)
+                for j in range(OUT_TILES):
+                    features = slice(j * P, (j + 1) * P)
+                    y_bank = psum.tile([P, CHUNK], F32, tag="bank")
+                    nc.tensor.matmul_mx(
+                        out=y_bank[:],
+                        lhsT=u_codes[:, features].bitcast(FP8X4),
+                        lhsT_scale=u_scales[:, features],
+                        rhs=h_codes[:].bitcast(FP8X4),
+                        rhs_scale=h_scales[:],
+                        start=True,
+                        stop=True,
+                    )
+                    u1_column = columns[:, U1_COL[b] + j : U1_COL[b] + j + 1]
+                    if b == 0:
+                        nc.scalar.activation(
+                            out=y_t[:, j, :],
+                            in_=y_bank[:],
+                            func=ACT.Identity,
+                            scale=u1_column,
+                            bias=columns[:, BIAS_COL + j : BIAS_COL + j + 1],
+                        )
+                    else:
+                        nc.scalar.activation(out=y_t[:, j, :], in_=y_bank[:], func=ACT.Copy, scale=u1_column)
+                y_scaled[(c, b)] = y_t
+
+        def store_out(c):
+            if not in_range(c):
+                return
+            out_tile = out_pool.tile([P, ROW_TILES, OUT_F], F32)
+            for half in range(2):
+                out_bank = psum.tile([P, 2, OUT_F], F32, tag="bank")
+                for i in range(2):
+                    columns_of_tile = slice((2 * half + i) * P, (2 * half + i + 1) * P)
+                    for j in range(OUT_TILES):
+                        for b in range(BRANCHES):
+                            nc.tensor.matmul(
+                                out=out_bank[:, i, j * P : (j + 1) * P],
+                                lhsT=y_scaled[(c, b)][:, j, columns_of_tile],
+                                rhs=ident_f32[:],
+                                is_transpose=True,
+                                start=(b == 0),
+                                stop=(b == BRANCHES - 1),
+                            )
+                nc.scalar.copy(out=out_tile[:, 2 * half : 2 * half + 2, :], in_=out_bank[:])
+            nc.sync.dma_start(
+                out=out_rows[c * CHUNK : (c + 1) * CHUNK, :].rearrange("(p i) o -> p i o", i=ROW_TILES),
+                in_=out_tile[:],
+            )
+
+        transpose_x(0)
+        scale_x(0)
+        for b in range(BRANCHES):
+            quantise_x(0, b)
+
+        vector_bank = psum.tile([P, P], BF16, tag="bank")
+        nc.tensor.transpose(vector_bank[:], vector_rows[:], ident_bf16[:])
+        columns = const.tile([P, N_COLUMNS], F32)
+        nc.vector.tensor_copy(out=columns[:], in_=vector_bank[:, 0:N_COLUMNS])
+        hidden_scale = const.tile([P, BRANCHES, HID_TILES], F32)
+        v1_and_u2 = columns[:, V1_COL[0] : V1_COL[1] + 2 * HID_TILES].rearrange(
+            "p (b v t) -> p b v t", b=BRANCHES, v=2
+        )
+        nc.vector.tensor_tensor(out=hidden_scale[:], in0=v1_and_u2[:, :, 0, :], in1=v1_and_u2[:, :, 1, :], op=ALU.mult)
+
+        for b in range(BRANCHES):
+            v_words = v_in[b][:].bitcast(F32)
+            v_signs = weight_stage.tile([P, X_PASSES, HID_F, PACK], BF16, align_bytes=64)
+            for g in range(X_PASSES):
+                for half in range(2):
+                    v_bank = psum.tile([P, 2, HALF], F32, tag="bank")
+                    for u in range(2):
+                        words = slice((2 * g + u) * P, (2 * g + u + 1) * P)
+                        for i in range(2):
+                            nc.tensor.transpose(
+                                v_bank[:, u, i * P : (i + 1) * P], v_words[:, 2 * half + i, words], ident_f32[:]
+                            )
+                    nc.scalar.activation(
+                        out=v_signs[:, g, half * HALF : (half + 1) * HALF, :].rearrange(
+                            "p c (u e) -> p c u e", e=PAIR
+                        ),
+                        in_=v_bank[:].bitcast(BF16).rearrange("p u (c e) -> p c u e", e=PAIR),
+                        func=ACT.Sign,
+                    )
+            v_codes = const.tile([P, X_PASSES, HID_F], U32, align_bytes=64, name="v_codes%d" % b)
+            v_scales = const.tile([P, X_PASSES, HID_F], U8, align_bytes=64, name="v_scales%d" % b)
+            nc.vector.quantize_mx(
+                out=v_codes[:].rearrange("p g s -> p (g s)").bitcast(FP8X4),
+                scales=v_scales[:].rearrange("p g s -> p (g s)"),
+                in_=v_signs[:].rearrange("p g s t -> p (g s t)"),
+            )
+            v_mx.append((v_codes, v_scales))
+
+        for b in range(BRANCHES):
+            u_bank = psum.tile([P, PACK, OUT_F], BF16, tag="bank")
+            for t in range(PACK):
+                for j in range(OUT_TILES):
+                    nc.tensor.transpose(
+                        u_bank[:, t, j * P : (j + 1) * P], u_in[b][:, j, t * P : (t + 1) * P], ident_bf16[:]
+                    )
+            u_signs = weight_stage.tile([P, OUT_F, PACK], BF16, align_bytes=64)
+            nc.scalar.activation(out=u_signs[:], in_=u_bank[:].rearrange("p t o -> p o t"), func=ACT.Sign)
+            u_codes = const.tile([P, OUT_F], U32, align_bytes=64, name="u_codes%d" % b)
+            u_scales = const.tile([P, OUT_F], U8, align_bytes=64, name="u_scales%d" % b)
+            nc.vector.quantize_mx(
+                out=u_codes[:].bitcast(FP8X4), scales=u_scales[:], in_=u_signs[:].rearrange("p o t -> p (o t)")
+            )
+            u_mx.append((u_codes, u_scales))
+
+        transpose_x(1)
+
+        for c in range(N_CHUNKS + 1):
+            first_product(c)
+            second_product(c - 1)
+            transpose_x(c + 2)
+            store_out(c - 1)
+            scale_x(c + 1)
+            group_h(c, 0)
+            quantise_x(c + 1, 0)
+            group_h(c, 1)
+            quantise_x(c + 1, 1)
+            quantise_h(c, 0)
+            quantise_h(c, 1)

@@ -56,6 +56,7 @@ def tile_littlebititqspeclinear_pa_t_kernel(
         x_psum = pools.enter_context(tc.psum_pool(name="x_psum", bufs=4))
         psum = pools.enter_context(tc.psum_pool(name="psum", bufs=4))
 
+        pools.enter_context(tc.manual_schedule())
         x_in = {}
 
         def load_x(c):
@@ -345,13 +346,13 @@ def tile_littlebititqspeclinear_pa_t_kernel(
 
         for c in range(N_CHUNKS + 1):
             first_product(c)
-            second_product(c - 1)
+            scale_x(c + 1)
             transpose_x(c + 2)
             store_out(c - 1)
-            scale_x(c + 1)
             group_h(c, 0)
-            quantise_x(c + 1, 0)
             group_h(c, 1)
-            quantise_x(c + 1, 1)
             quantise_h(c, 0)
             quantise_h(c, 1)
+            second_product(c)
+            quantise_x(c + 1, 0)
+            quantise_x(c + 1, 1)

@@ -56,7 +56,6 @@ def tile_littlebititqspeclinear_pa_t_kernel(
         x_psum = pools.enter_context(tc.psum_pool(name="x_psum", bufs=4))
         psum = pools.enter_context(tc.psum_pool(name="psum", bufs=4))
 
-        pools.enter_context(tc.manual_schedule())
         x_in = {}
 
         def load_x(c):
@@ -205,10 +204,20 @@ def tile_littlebititqspeclinear_pa_t_kernel(
             if not in_range(c):
                 return
             grouped = one_chunk.tile([P, CHUNK, PACK], BF16, align_bytes=64)
-            nc.vector.tensor_copy(
-                out=grouped[:].rearrange("p (c i) t -> p c t i", i=4),
-                in_=h_planes[(c, b)][:].rearrange("p t (c i) -> p c t i", i=4),
-            )
+            if b == 0:
+                nc.gpsimd.tensor_scalar(
+                    out=grouped[:],
+                    in0=h_planes[(c, b)][:].rearrange("p t c -> p c t"),
+                    scalar1=1.0,
+                    scalar2=0.0,
+                    op0=ALU.mult,
+                    op1=ALU.add,
+                )
+            else:
+                nc.vector.tensor_copy(
+                    out=grouped[:].rearrange("p (c i) t -> p c t i", i=4),
+                    in_=h_planes[(c, b)][:].rearrange("p t (c i) -> p c t i", i=4),
+                )
             h_grouped[(c, b)] = grouped
 
         h_mx = {}
@@ -346,13 +355,13 @@ def tile_littlebititqspeclinear_pa_t_kernel(
 
         for c in range(N_CHUNKS + 1):
             first_product(c)
-            scale_x(c + 1)
+            second_product(c - 1)
             transpose_x(c + 2)
             store_out(c - 1)
+            scale_x(c + 1)
             group_h(c, 0)
+            quantise_x(c + 1, 0)
             group_h(c, 1)
+            quantise_x(c + 1, 1)
             quantise_h(c, 0)
             quantise_h(c, 1)
-            second_product(c)
-            quantise_x(c + 1, 0)
-            quantise_x(c + 1, 1)

@@ -23,12 +23,13 @@ OUT_F = 256
 BRANCHES = 2
 
 CHUNK = 512
-N_CHUNKS = ROWS // CHUNK
-ROW_TILES = CHUNK // P
+HALF = 256
+WIDTHS = [HALF] + [CHUNK] * (ROWS // CHUNK - 1) + [HALF]
+FIRST_ROWS = [sum(WIDTHS[:c]) for c in range(len(WIDTHS))]
+N_CHUNKS = len(WIDTHS)
 X_PASSES = IN_F // K_PASS
 HID_TILES = HID_F // P
 OUT_TILES = OUT_F // P
-HALF = 256
 assert HID_F == K_PASS and HID_TILES == PACK
 
 V1_COL = (0, 8)
@@ -47,41 +48,45 @@ def tile_littlebititqspeclinear_pa_t_kernel(
     out_rows = out.flatten_outer_dims()
 
     with ExitStack() as pools:
+        pools.enter_context(tc.manual_schedule())
         const = pools.enter_context(tc.tile_pool(name="const", bufs=1))
         weight_stage = pools.enter_context(tc.tile_pool(name="weight_stage", bufs=2))
-        x_pool = pools.enter_context(tc.tile_pool(name="x_pool", bufs=N_CHUNKS))
+        x_pool = pools.enter_context(tc.tile_pool(name="x_pool", bufs=8))
         one_chunk = pools.enter_context(tc.tile_pool(name="one_chunk", bufs=BRANCHES))
         two_chunks = pools.enter_context(tc.tile_pool(name="two_chunks", bufs=2 * BRANCHES))
+        three_chunks = pools.enter_context(tc.tile_pool(name="three_chunks", bufs=3 * BRANCHES))
         out_pool = pools.enter_context(tc.tile_pool(name="out_pool", bufs=2))
         x_psum = pools.enter_context(tc.psum_pool(name="x_psum", bufs=4))
         psum = pools.enter_context(tc.psum_pool(name="psum", bufs=4))
 
         x_in = {}
 
+        def rows_of(dram, c):
+            chunk = dram[FIRST_ROWS[c] : FIRST_ROWS[c] + WIDTHS[c], :]
+            return chunk.rearrange("(p i) k -> p i k", i=WIDTHS[c] // P)
+
         def load_x(c):
-            x_tile = x_pool.tile([P, ROW_TILES, IN_F], BF16)
-            source = x_rows[c * CHUNK : (c + 1) * CHUNK, :].rearrange("(p i) k -> p i k", i=ROW_TILES)
-            for half in range(2):
-                tiles = slice(half * 2, half * 2 + 2)
+            x_tile = x_pool.tile([P, WIDTHS[c] // P, IN_F], BF16)
+            source = rows_of(x_rows, c)
+            n_loads = 2 if c == 1 else 1
+            for half in range(n_loads):
+                n_tiles = WIDTHS[c] // P // n_loads
+                tiles = slice(half * n_tiles, (half + 1) * n_tiles)
                 nc.sync.dma_start(out=x_tile[:, tiles, :], in_=source[:, tiles, :])
             x_in[c] = x_tile
 
+        table_probe = const.tile([P, 1], F32)
+        nc.vector.memset(table_probe[:], 0.0)
+        nc.scalar.activation(out=table_probe[:], in_=table_probe[:], func=ACT.Sign)
+
         v2_rows = const.tile([P, PAIR * P], BF16)
-        nc.vector.memset(v2_rows[:], 0.0)
+        nc.gpsimd.memset(v2_rows[:], 0.0)
         for b, vector in enumerate((v2, v2_R)):
-            nc.scalar.dma_start(
+            nc.sync.dma_start(
                 out=v2_rows[4 * b : 4 * b + 4, :], in_=vector.rearrange("o (f w) -> (o f) w", w=PAIR * P)
             )
-        load_x(0)
-
-        v_in = []
-        for weight in (V, V_R):
-            v_tile = weight_stage.tile([P, HID_TILES, IN_F], BF16)
-            nc.sync.dma_start(out=v_tile[:], in_=weight.rearrange("(m p) k -> p m k", p=P))
-            v_in.append(v_tile)
-
         vector_rows = const.tile([P, P], BF16)
-        nc.vector.memset(vector_rows[:], 0.0)
+        nc.gpsimd.memset(vector_rows[:], 0.0)
         first_row = 0
         for vector in (v1, u2, v1_R, u2_R, u1, u1_R):
             n_rows = vector.shape[1] // P
@@ -93,27 +98,37 @@ def tile_littlebititqspeclinear_pa_t_kernel(
             out=vector_rows[BIAS_COL : BIAS_COL + OUT_TILES, :], in_=bias.rearrange("(j p) -> j p", p=P)
         )
 
-        u_in = []
-        for weight in (U, U_R):
-            u_tile = weight_stage.tile([P, OUT_TILES, HID_F], BF16)
-            nc.scalar.dma_start(out=u_tile[:], in_=weight.rearrange("(j p) s -> p j s", p=P))
-            u_in.append(u_tile)
-
-        for c in range(1, N_CHUNKS):
-            load_x(c)
-
         ident_f32 = const.tile([P, P], F32)
         make_identity(nc, ident_f32[:])
         ident_bf16 = const.tile([P, P], BF16)
         make_identity(nc, ident_bf16[:])
 
+        v_in = []
+
+        def load_v(weight):
+            v_tile = weight_stage.tile([P, HID_TILES, IN_F], BF16)
+            source = weight.rearrange("(m p) k -> p m k", p=P)
+            for half in range(2):
+                tiles = slice(half * 2, half * 2 + 2)
+                nc.sync.dma_start(out=v_tile[:, tiles, :], in_=source[:, tiles, :])
+            v_in.append(v_tile)
+
+        load_x(0)
+        load_v(V)
+        load_x(1)
+        load_v(V_R)
+        u_in = []
+        for weight in (U, U_R):
+            u_tile = weight_stage.tile([P, OUT_TILES, HID_F], BF16)
+            nc.sync.dma_start(out=u_tile[:], in_=weight.rearrange("(j p) s -> p j s", p=P))
+            u_in.append(u_tile)
+        for c in range(2, N_CHUNKS):
+            load_x(c)
+
         def in_range(c):
             return 0 <= c < N_CHUNKS
 
-        v2_bank = psum.tile([P, P], F32, tag="bank")
-        nc.tensor.transpose(v2_bank[:], v2_rows[:].bitcast(F32), ident_f32[:])
         v2_words = const.tile([P, BRANCHES * X_PASSES * 2], F32)
-        nc.vector.tensor_copy(out=v2_words[:], in_=v2_bank[:, 0 : BRANCHES * X_PASSES * 2])
         v2_values = v2_words[:].bitcast(BF16).rearrange("p (b g t) -> p b g t", b=BRANCHES, g=X_PASSES)
 
         x_banks = {}
@@ -123,7 +138,7 @@ def tile_littlebititqspeclinear_pa_t_kernel(
                 return
             x_words = x_in[c][:].bitcast(F32)
             x_banks[c] = []
-            for half in range(2):
+            for half in range(WIDTHS[c] // HALF):
                 for g in range(X_PASSES):
                     x_bank = x_psum.tile([P, 2, HALF], F32)
                     for u in range(2):
@@ -136,15 +151,17 @@ def tile_littlebititqspeclinear_pa_t_kernel(
 
         x_scaled = {}
 
-        def scale_x(c):
+        def scale_x(c, halves=(0, 1)):
             if not in_range(c):
                 return
-            for b in range(BRANCHES):
-                scaled = one_chunk.tile([P, X_PASSES, CHUNK, PACK], BF16, align_bytes=64)
-                x_scaled[(c, b)] = scaled
             for half, g, x_bank in x_banks[c]:
+                if half not in halves:
+                    continue
                 columns_of_half = slice(half * HALF, (half + 1) * HALF)
                 for b in range(BRANCHES):
+                    if (c, b) not in x_scaled:
+                        scaled = one_chunk.tile([P, X_PASSES, WIDTHS[c], PACK], BF16, align_bytes=64)
+                        x_scaled[(c, b)] = scaled
                     nc.vector.tensor_tensor(
                         out=x_scaled[(c, b)][:, g, columns_of_half, :].rearrange("p c (u e) -> p c u e", e=PAIR),
                         in0=x_bank[:].bitcast(BF16).rearrange("p u (c e) -> p c u e", e=PAIR),
@@ -160,8 +177,8 @@ def tile_littlebititqspeclinear_pa_t_kernel(
         def quantise_x(c, b):
             if not in_range(c):
                 return
-            x_codes = two_chunks.tile([P, X_PASSES, CHUNK], U32, align_bytes=64)
-            x_scales = two_chunks.tile([P, X_PASSES, CHUNK], U8, align_bytes=64)
+            x_codes = two_chunks.tile([P, X_PASSES, WIDTHS[c]], U32, align_bytes=64)
+            x_scales = two_chunks.tile([P, X_PASSES, WIDTHS[c]], U8, align_bytes=64)
             nc.vector.quantize_mx(
                 out=x_codes[:].rearrange("p g c -> p (g c)").bitcast(FP8X4),
                 scales=x_scales[:].rearrange("p g c -> p (g c)"),
@@ -173,16 +190,16 @@ def tile_littlebititqspeclinear_pa_t_kernel(
         u_mx = []
         h_planes = {}
 
-        def first_product(c):
+        def first_product(c, branches=(0, 1)):
             if not in_range(c):
                 return
-            for b in range(BRANCHES):
+            for b in branches:
                 v_codes, v_scales = v_mx[b]
                 x_codes, x_scales = x_mx[(c, b)]
-                h_plane = two_chunks.tile([P, HID_TILES, CHUNK], BF16)
+                h_plane = three_chunks.tile([P, HID_TILES, WIDTHS[c]], BF16)
                 for t in range(HID_TILES):
                     features = slice(t * P, (t + 1) * P)
-                    h_bank = psum.tile([P, CHUNK], F32, tag="bank")
+                    h_bank = psum.tile([P, WIDTHS[c]], F32, tag="bank")
                     for g in range(X_PASSES):
                         nc.tensor.matmul_mx(
                             out=h_bank[:],
@@ -200,11 +217,11 @@ def tile_littlebititqspeclinear_pa_t_kernel(
 
         h_grouped = {}
 
-        def group_h(c, b):
+        def group_h(c, b, engine):
             if not in_range(c):
                 return
-            grouped = one_chunk.tile([P, CHUNK, PACK], BF16, align_bytes=64)
-            if b == 0:
+            grouped = one_chunk.tile([P, WIDTHS[c], PACK], BF16, align_bytes=64)
+            if engine == "gpsimd":
                 nc.gpsimd.tensor_scalar(
                     out=grouped[:],
                     in0=h_planes[(c, b)][:].rearrange("p t c -> p c t"),
@@ -225,8 +242,8 @@ def tile_littlebititqspeclinear_pa_t_kernel(
         def quantise_h(c, b):
             if not in_range(c):
                 return
-            h_codes = two_chunks.tile([P, CHUNK], U32, align_bytes=64)
-            h_scales = two_chunks.tile([P, CHUNK], U8, align_bytes=64)
+            h_codes = two_chunks.tile([P, WIDTHS[c]], U32, align_bytes=64)
+            h_scales = two_chunks.tile([P, WIDTHS[c]], U8, align_bytes=64)
             nc.vector.quantize_mx(
                 out=h_codes[:].bitcast(FP8X4),
                 scales=h_scales[:],
@@ -236,16 +253,16 @@ def tile_littlebititqspeclinear_pa_t_kernel(
 
         y_scaled = {}
 
-        def second_product(c):
+        def second_product(c, branches=(0, 1), engine="scalar"):
             if not in_range(c):
                 return
-            for b in range(BRANCHES):
+            for b in branches:
                 u_codes, u_scales = u_mx[b]
                 h_codes, h_scales = h_mx[(c, b)]
-                y_t = two_chunks.tile([P, OUT_TILES, CHUNK], F32)
+                y_t = two_chunks.tile([P, OUT_TILES, WIDTHS[c]], F32)
                 for j in range(OUT_TILES):
                     features = slice(j * P, (j + 1) * P)
-                    y_bank = psum.tile([P, CHUNK], F32, tag="bank")
+                    y_bank = psum.tile([P, WIDTHS[c]], F32, tag="bank")
                     nc.tensor.matmul_mx(
                         out=y_bank[:],
                         lhsT=u_codes[:, features].bitcast(FP8X4),
@@ -264,15 +281,19 @@ def tile_littlebititqspeclinear_pa_t_kernel(
                             scale=u1_column,
                             bias=columns[:, BIAS_COL + j : BIAS_COL + j + 1],
                         )
-                    else:
+                    elif engine == "scalar":
                         nc.scalar.activation(out=y_t[:, j, :], in_=y_bank[:], func=ACT.Copy, scale=u1_column)
+                    else:
+                        nc.vector.tensor_scalar(
+                            out=y_t[:, j, :], in0=y_bank[:], scalar1=u1_column, scalar2=None, op0=ALU.mult
+                        )
                 y_scaled[(c, b)] = y_t
 
-        def store_out(c):
+        def store_out(c, engines=("scalar", "scalar")):
             if not in_range(c):
                 return
-            out_tile = out_pool.tile([P, ROW_TILES, OUT_F], F32)
-            for half in range(2):
+            out_tile = out_pool.tile([P, WIDTHS[c] // P, OUT_F], F32)
+            for half in range(WIDTHS[c] // HALF):
                 out_bank = psum.tile([P, 2, OUT_F], F32, tag="bank")
                 for i in range(2):
                     columns_of_tile = slice((2 * half + i) * P, (2 * half + i + 1) * P)
@@ -286,32 +307,22 @@ def tile_littlebititqspeclinear_pa_t_kernel(
                                 start=(b == 0),
                                 stop=(b == BRANCHES - 1),
                             )
-                nc.scalar.copy(out=out_tile[:, 2 * half : 2 * half + 2, :], in_=out_bank[:])
-            nc.sync.dma_start(
-                out=out_rows[c * CHUNK : (c + 1) * CHUNK, :].rearrange("(p i) o -> p i o", i=ROW_TILES),
-                in_=out_tile[:],
-            )
+                if engines[half] == "scalar":
+                    nc.scalar.copy(out=out_tile[:, 2 * half : 2 * half + 2, :], in_=out_bank[:])
+                else:
+                    nc.vector.tensor_copy(out=out_tile[:, 2 * half : 2 * half + 2, :], in_=out_bank[:])
+            nc.sync.dma_start(out=rows_of(out_rows, c), in_=out_tile[:])
 
-        transpose_x(0)
-        scale_x(0)
-        for b in range(BRANCHES):
-            quantise_x(0, b)
+        v_signs_of = {}
 
-        vector_bank = psum.tile([P, P], BF16, tag="bank")
-        nc.tensor.transpose(vector_bank[:], vector_rows[:], ident_bf16[:])
-        columns = const.tile([P, N_COLUMNS], F32)
-        nc.vector.tensor_copy(out=columns[:], in_=vector_bank[:, 0:N_COLUMNS])
-        hidden_scale = const.tile([P, BRANCHES, HID_TILES], F32)
-        v1_and_u2 = columns[:, V1_COL[0] : V1_COL[1] + 2 * HID_TILES].rearrange(
-            "p (b v t) -> p b v t", b=BRANCHES, v=2
-        )
-        nc.vector.tensor_tensor(out=hidden_scale[:], in0=v1_and_u2[:, :, 0, :], in1=v1_and_u2[:, :, 1, :], op=ALU.mult)
-
-        for b in range(BRANCHES):
+        def sign_v(b, halves=(0, 1)):
             v_words = v_in[b][:].bitcast(F32)
-            v_signs = weight_stage.tile([P, X_PASSES, HID_F, PACK], BF16, align_bytes=64)
-            for g in range(X_PASSES):
-                for half in range(2):
+            if b not in v_signs_of:
+                v_signs = weight_stage.tile([P, X_PASSES, HID_F, PACK], BF16, align_bytes=64)
+                v_signs_of[b] = v_signs
+            v_signs = v_signs_of[b]
+            for half in halves:
+                for g in range(X_PASSES):
                     v_bank = psum.tile([P, 2, HALF], F32, tag="bank")
                     for u in range(2):
                         words = slice((2 * g + u) * P, (2 * g + u + 1) * P)
@@ -326,16 +337,20 @@ def tile_littlebititqspeclinear_pa_t_kernel(
                         in_=v_bank[:].bitcast(BF16).rearrange("p u (c e) -> p c u e", e=PAIR),
                         func=ACT.Sign,
                     )
+
+        def quantise_v(b):
             v_codes = const.tile([P, X_PASSES, HID_F], U32, align_bytes=64, name="v_codes%d" % b)
             v_scales = const.tile([P, X_PASSES, HID_F], U8, align_bytes=64, name="v_scales%d" % b)
             nc.vector.quantize_mx(
                 out=v_codes[:].rearrange("p g s -> p (g s)").bitcast(FP8X4),
                 scales=v_scales[:].rearrange("p g s -> p (g s)"),
-                in_=v_signs[:].rearrange("p g s t -> p (g s t)"),
+                in_=v_signs_of[b][:].rearrange("p g s t -> p (g s t)"),
             )
             v_mx.append((v_codes, v_scales))
 
-        for b in range(BRANCHES):
+        u_signs_of = {}
+
+        def sign_u(b):
             u_bank = psum.tile([P, PACK, OUT_F], BF16, tag="bank")
             for t in range(PACK):
                 for j in range(OUT_TILES):
@@ -344,24 +359,69 @@ def tile_littlebititqspeclinear_pa_t_kernel(
                     )
             u_signs = weight_stage.tile([P, OUT_F, PACK], BF16, align_bytes=64)
             nc.scalar.activation(out=u_signs[:], in_=u_bank[:].rearrange("p t o -> p o t"), func=ACT.Sign)
+            u_signs_of[b] = u_signs
+
+        def quantise_u(b):
             u_codes = const.tile([P, OUT_F], U32, align_bytes=64, name="u_codes%d" % b)
             u_scales = const.tile([P, OUT_F], U8, align_bytes=64, name="u_scales%d" % b)
             nc.vector.quantize_mx(
-                out=u_codes[:].bitcast(FP8X4), scales=u_scales[:], in_=u_signs[:].rearrange("p o t -> p (o t)")
+                out=u_codes[:].bitcast(FP8X4), scales=u_scales[:], in_=u_signs_of[b][:].rearrange("p o t -> p (o t)")
             )
             u_mx.append((u_codes, u_scales))
 
-        transpose_x(1)
+        v2_bank = psum.tile([P, P], F32, tag="bank")
+        nc.tensor.transpose(v2_bank[:], v2_rows[:].bitcast(F32), ident_f32[:])
+        nc.vector.tensor_copy(out=v2_words[:], in_=v2_bank[:, 0 : BRANCHES * X_PASSES * 2])
 
-        for c in range(N_CHUNKS + 1):
-            first_product(c)
-            second_product(c - 1)
-            transpose_x(c + 2)
-            store_out(c - 1)
-            scale_x(c + 1)
-            group_h(c, 0)
-            quantise_x(c + 1, 0)
-            group_h(c, 1)
-            quantise_x(c + 1, 1)
-            quantise_h(c, 0)
+        transpose_x(0)
+        scale_x(0)
+        sign_v(0, (0,))
+
+        vector_bank = psum.tile([P, P], BF16, tag="bank")
+        nc.tensor.transpose(vector_bank[:], vector_rows[:], ident_bf16[:])
+        columns = const.tile([P, N_COLUMNS], F32)
+        nc.vector.tensor_copy(out=columns[:], in_=vector_bank[:, 0:N_COLUMNS])
+        hidden_scale = const.tile([P, BRANCHES, HID_TILES], F32)
+        v1_and_u2 = columns[:, V1_COL[0] : V1_COL[1] + 2 * HID_TILES].rearrange(
+            "p (b v t) -> p b v t", b=BRANCHES, v=2
+        )
+
+        sign_v(0, (1,))
+        quantise_x(0, 0)
+        nc.vector.tensor_tensor(out=hidden_scale[:], in0=v1_and_u2[:, :, 0, :], in1=v1_and_u2[:, :, 1, :], op=ALU.mult)
+        quantise_x(0, 1)
+        transpose_x(1)
+        scale_x(1, (0,))
+        quantise_v(0)
+        scale_x(1, (1,))
+        sign_v(1, (0,))
+        first_product(0, (0,))
+        sign_v(1, (1,))
+        transpose_x(2)
+        quantise_x(1, 0)
+        quantise_v(1)
+        quantise_x(1, 1)
+        first_product(0, (1,))
+        for b in range(BRANCHES):
+            sign_u(b)
+        first_product(1)
+
+        for c in range(N_CHUNKS):
+            group_h(c, 0, "gpsimd" if c < N_CHUNKS - 2 else "vector")
+            scale_x(c + 2)
+            transpose_x(c + 3)
+            if c == 0:
+                for b in range(BRANCHES):
+                    quantise_u(b)
+            for b in range(BRANCHES):
+                quantise_x(c + 2, b)
+                first_product(c + 2, (b,))
+            group_h(c, 1, "vector")
             quantise_h(c, 1)
+            quantise_h(c, 0)
+            second_product(c, (0,))
+            second_product(c, (1,), "scalar" if c < N_CHUNKS - 1 else "vector")
+            if c < N_CHUNKS - 1:
+                store_out(c - 1)
+        store_out(N_CHUNKS - 2, ("scalar", "vector"))
+        store_out(N_CHUNKS - 1, ("vector",))

@@ -217,14 +217,18 @@ def tile_littlebititqspeclinear_pa_t_kernel(
 
         h_grouped = {}
 
-        def group_h(c, b, engine):
+        def group_h(c, b, engine, first=0, last=CHUNK):
             if not in_range(c):
                 return
-            grouped = one_chunk.tile([P, WIDTHS[c], PACK], BF16, align_bytes=64)
+            if (c, b) not in h_grouped:
+                grouped = one_chunk.tile([P, WIDTHS[c], PACK], BF16, align_bytes=64)
+                h_grouped[(c, b)] = grouped
+            grouped = h_grouped[(c, b)]
+            columns_here = slice(first, min(last, WIDTHS[c]))
             if engine == "gpsimd":
                 nc.gpsimd.tensor_scalar(
-                    out=grouped[:],
-                    in0=h_planes[(c, b)][:].rearrange("p t c -> p c t"),
+                    out=grouped[:, columns_here, :],
+                    in0=h_planes[(c, b)][:, :, columns_here].rearrange("p t c -> p c t"),
                     scalar1=1.0,
                     scalar2=0.0,
                     op0=ALU.mult,
@@ -232,10 +236,9 @@ def tile_littlebititqspeclinear_pa_t_kernel(
                 )
             else:
                 nc.vector.tensor_copy(
-                    out=grouped[:].rearrange("p (c i) t -> p c t i", i=4),
-                    in_=h_planes[(c, b)][:].rearrange("p t (c i) -> p c t i", i=4),
+                    out=grouped[:, columns_here, :].rearrange("p (c i) t -> p c t i", i=4),
+                    in_=h_planes[(c, b)][:, :, columns_here].rearrange("p t (c i) -> p c t i", i=4),
                 )
-            h_grouped[(c, b)] = grouped
 
         h_mx = {}
 
@@ -394,34 +397,55 @@ def tile_littlebititqspeclinear_pa_t_kernel(
         scale_x(1, (0,))
         quantise_v(0)
         scale_x(1, (1,))
-        sign_v(1, (0,))
+        sign_v(1)
         first_product(0, (0,))
-        sign_v(1, (1,))
         transpose_x(2)
         quantise_x(1, 0)
         quantise_v(1)
         quantise_x(1, 1)
         first_product(0, (1,))
+        group_h(0, 0, "gpsimd")
+        scale_x(2, (0,))
+        first_product(1, (0,))
         for b in range(BRANCHES):
             sign_u(b)
-        first_product(1)
+        first_product(1, (1,))
+        group_h(0, 1, "vector")
+        quantise_h(0, 1)
+        quantise_h(0, 0)
+        group_h(1, 0, "gpsimd")
+        scale_x(2, (1,))
+        for b in range(BRANCHES):
+            quantise_u(b)
+        second_product(0)
+        transpose_x(3)
+        for b in range(BRANCHES):
+            quantise_x(2, b)
+            first_product(2, (b,))
+        group_h(1, 1, "vector")
+        quantise_h(1, 1)
+        quantise_h(1, 0)
+        second_product(1)
+        store_out(0)
 
-        for c in range(N_CHUNKS):
-            group_h(c, 0, "gpsimd" if c < N_CHUNKS - 2 else "vector")
-            scale_x(c + 2)
-            transpose_x(c + 3)
-            if c == 0:
-                for b in range(BRANCHES):
-                    quantise_u(b)
+        for c in range(2, N_CHUNKS):
+            last_turn = c == N_CHUNKS - 1
+            group_h(c, 0, "vector" if last_turn else "gpsimd")
+            if not last_turn:
+                group_h(c, 1, "gpsimd", 0, WIDTHS[c] // 2)
+            scale_x(c + 1)
+            transpose_x(c + 2)
             for b in range(BRANCHES):
-                quantise_x(c + 2, b)
-                first_product(c + 2, (b,))
-            group_h(c, 1, "vector")
+                quantise_x(c + 1, b)
+                first_product(c + 1, (b,))
+            group_h(c, 1, "vector", 0 if last_turn else WIDTHS[c] // 2)
             quantise_h(c, 1)
             quantise_h(c, 0)
+            if last_turn:
+                store_out(c - 2, ("vector", "vector"))
             second_product(c, (0,))
-            second_product(c, (1,), "scalar" if c < N_CHUNKS - 1 else "vector")
-            if c < N_CHUNKS - 1:
+            second_product(c, (1,), "vector" if last_turn else "scalar")
+            if c < N_CHUNKS - 2:
                 store_out(c - 1)
         store_out(N_CHUNKS - 2, ("scalar", "vector"))
         store_out(N_CHUNKS - 1, ("vector",))

@@ -54,7 +54,6 @@ def tile_littlebititqspeclinear_pa_t_kernel(
         x_pool = pools.enter_context(tc.tile_pool(name="x_pool", bufs=8))
         one_chunk = pools.enter_context(tc.tile_pool(name="one_chunk", bufs=BRANCHES))
         two_chunks = pools.enter_context(tc.tile_pool(name="two_chunks", bufs=2 * BRANCHES))
-        three_chunks = pools.enter_context(tc.tile_pool(name="three_chunks", bufs=3 * BRANCHES))
         out_pool = pools.enter_context(tc.tile_pool(name="out_pool", bufs=2))
         x_psum = pools.enter_context(tc.psum_pool(name="x_psum", bufs=4))
         psum = pools.enter_context(tc.psum_pool(name="psum", bufs=4))
@@ -190,14 +189,15 @@ def tile_littlebititqspeclinear_pa_t_kernel(
         u_mx = []
         h_planes = {}
 
-        def first_product(c, branches=(0, 1)):
-            if not in_range(c):
-                return
-            for b in branches:
+        def first_product(c, b, tiles=range(HID_TILES)):
+            if in_range(c):
                 v_codes, v_scales = v_mx[b]
                 x_codes, x_scales = x_mx[(c, b)]
-                h_plane = three_chunks.tile([P, HID_TILES, WIDTHS[c]], BF16)
-                for t in range(HID_TILES):
+                if (c, b) not in h_planes:
+                    h_plane = two_chunks.tile([P, HID_TILES, WIDTHS[c]], BF16)
+                    h_planes[(c, b)] = h_plane
+                h_plane = h_planes[(c, b)]
+                for t in tiles:
                     features = slice(t * P, (t + 1) * P)
                     h_bank = psum.tile([P, WIDTHS[c]], F32, tag="bank")
                     for g in range(X_PASSES):
@@ -213,7 +213,6 @@ def tile_littlebititqspeclinear_pa_t_kernel(
                     nc.scalar.activation(
                         out=h_plane[:, t, :], in_=h_bank[:], func=ACT.Copy, scale=hidden_scale[:, b, t : t + 1]
                     )
-                h_planes[(c, b)] = h_plane
 
         h_grouped = {}
 
@@ -398,54 +397,52 @@ def tile_littlebititqspeclinear_pa_t_kernel(
         quantise_v(0)
         scale_x(1, (1,))
         sign_v(1)
-        first_product(0, (0,))
+        first_product(0, 0)
         transpose_x(2)
         quantise_x(1, 0)
         quantise_v(1)
         quantise_x(1, 1)
-        first_product(0, (1,))
-        group_h(0, 0, "gpsimd")
-        scale_x(2, (0,))
-        first_product(1, (0,))
+        first_product(0, 1)
         for b in range(BRANCHES):
             sign_u(b)
-        first_product(1, (1,))
-        group_h(0, 1, "vector")
-        quantise_h(0, 1)
-        quantise_h(0, 0)
-        group_h(1, 0, "gpsimd")
-        scale_x(2, (1,))
-        for b in range(BRANCHES):
-            quantise_u(b)
-        second_product(0)
-        transpose_x(3)
-        for b in range(BRANCHES):
-            quantise_x(2, b)
-            first_product(2, (b,))
-        group_h(1, 1, "vector")
-        quantise_h(1, 1)
-        quantise_h(1, 0)
-        second_product(1)
-        store_out(0)
 
-        for c in range(2, N_CHUNKS):
-            last_turn = c == N_CHUNKS - 1
-            group_h(c, 0, "vector" if last_turn else "gpsimd")
-            if not last_turn:
-                group_h(c, 1, "gpsimd", 0, WIDTHS[c] // 2)
-            scale_x(c + 1)
-            transpose_x(c + 2)
+        for c in range(N_CHUNKS - 2):
+            group_h(c, 0, "gpsimd")
+            on_gpsimd = WIDTHS[c] // 2 if WIDTHS[c + 2] == CHUNK else 0
+            if on_gpsimd > 0:
+                group_h(c, 1, "gpsimd", 0, on_gpsimd)
+            scale_x(c + 2)
+            if c == 0:
+                for b in range(BRANCHES):
+                    quantise_u(b)
             for b in range(BRANCHES):
-                quantise_x(c + 1, b)
-                first_product(c + 1, (b,))
-            group_h(c, 1, "vector", 0 if last_turn else WIDTHS[c] // 2)
+                quantise_x(c + 2, b)
+            group_h(c, 1, "vector", on_gpsimd)
             quantise_h(c, 1)
             quantise_h(c, 0)
-            if last_turn:
-                store_out(c - 2, ("vector", "vector"))
-            second_product(c, (0,))
-            second_product(c, (1,), "vector" if last_turn else "scalar")
-            if c < N_CHUNKS - 2:
-                store_out(c - 1)
-        store_out(N_CHUNKS - 2, ("scalar", "vector"))
-        store_out(N_CHUNKS - 1, ("vector",))
+            second_product(c - 1)
+            first_product(c + 1, 0)
+            store_out(c - 1)
+            first_product(c + 1, 1, (0, 1))
+            transpose_x(c + 3)
+            first_product(c + 1, 1, (2, 3))
+
+        c = N_CHUNKS - 2
+        second_product(c - 1, (0,))
+        group_h(c, 0, "vector")
+        second_product(c - 1, (1,), "vector")
+        first_product(c + 1, 0)
+        group_h(c, 1, "vector")
+        quantise_h(c, 1)
+        quantise_h(c, 0)
+        store_out(c - 1, ("vector", "vector"))
+        first_product(c + 1, 1)
+        for b in range(BRANCHES):
+            group_h(c + 1, b, "vector")
+        for b in range(BRANCHES):
+            quantise_h(c + 1, b)
+        second_product(c)
+        second_product(c + 1, (0,))
+        second_product(c + 1, (1,), "vector")
+        store_out(c, ("scalar", "vector"))
+        store_out(c + 1, ("vector",))

@@ -189,7 +189,7 @@ def tile_littlebititqspeclinear_pa_t_kernel(
         u_mx = []
         h_planes = {}
 
-        def first_product(c, b, tiles=range(HID_TILES)):
+        def first_product(c, b, tiles=range(HID_TILES), engine="scalar"):
             if in_range(c):
                 v_codes, v_scales = v_mx[b]
                 x_codes, x_scales = x_mx[(c, b)]
@@ -210,9 +210,13 @@ def tile_littlebititqspeclinear_pa_t_kernel(
                             start=(g == 0),
                             stop=(g == X_PASSES - 1),
                         )
-                    nc.scalar.activation(
-                        out=h_plane[:, t, :], in_=h_bank[:], func=ACT.Copy, scale=hidden_scale[:, b, t : t + 1]
-                    )
+                    scale_column = hidden_scale[:, b, t : t + 1]
+                    if engine == "scalar":
+                        nc.scalar.activation(out=h_plane[:, t, :], in_=h_bank[:], func=ACT.Copy, scale=scale_column)
+                    else:
+                        nc.vector.tensor_scalar(
+                            out=h_plane[:, t, :], in0=h_bank[:], scalar1=scale_column, scalar2=None, op0=ALU.mult
+                        )
 
         h_grouped = {}
 
@@ -253,43 +257,47 @@ def tile_littlebititqspeclinear_pa_t_kernel(
             )
             h_mx[(c, b)] = (h_codes, h_scales)
 
-        y_scaled = {}
+        y_parts = {}
 
-        def second_product(c, branches=(0, 1), engine="scalar"):
+        def second_product(c, b, add_up=False):
             if not in_range(c):
                 return
-            for b in branches:
-                u_codes, u_scales = u_mx[b]
-                h_codes, h_scales = h_mx[(c, b)]
-                y_t = two_chunks.tile([P, OUT_TILES, WIDTHS[c]], F32)
-                for j in range(OUT_TILES):
-                    features = slice(j * P, (j + 1) * P)
-                    y_bank = psum.tile([P, WIDTHS[c]], F32, tag="bank")
-                    nc.tensor.matmul_mx(
-                        out=y_bank[:],
-                        lhsT=u_codes[:, features].bitcast(FP8X4),
-                        lhsT_scale=u_scales[:, features],
-                        rhs=h_codes[:].bitcast(FP8X4),
-                        rhs_scale=h_scales[:],
-                        start=True,
-                        stop=True,
+            u_codes, u_scales = u_mx[b]
+            h_codes, h_scales = h_mx[(c, b)]
+            y_t = two_chunks.tile([P, OUT_TILES, WIDTHS[c]], F32)
+            for j in range(OUT_TILES):
+                features = slice(j * P, (j + 1) * P)
+                y_bank = psum.tile([P, WIDTHS[c]], F32, tag="bank")
+                nc.tensor.matmul_mx(
+                    out=y_bank[:],
+                    lhsT=u_codes[:, features].bitcast(FP8X4),
+                    lhsT_scale=u_scales[:, features],
+                    rhs=h_codes[:].bitcast(FP8X4),
+                    rhs_scale=h_scales[:],
+                    start=True,
+                    stop=True,
+                )
+                u1_column = columns[:, U1_COL[b] + j : U1_COL[b] + j + 1]
+                if b == 0:
+                    nc.scalar.activation(
+                        out=y_t[:, j, :],
+                        in_=y_bank[:],
+                        func=ACT.Identity,
+                        scale=u1_column,
+                        bias=columns[:, BIAS_COL + j : BIAS_COL + j + 1],
                     )
-                    u1_column = columns[:, U1_COL[b] + j : U1_COL[b] + j + 1]
-                    if b == 0:
-                        nc.scalar.activation(
-                            out=y_t[:, j, :],
-                            in_=y_bank[:],
-                            func=ACT.Identity,
-                            scale=u1_column,
-                            bias=columns[:, BIAS_COL + j : BIAS_COL + j + 1],
-                        )
-                    elif engine == "scalar":
-                        nc.scalar.activation(out=y_t[:, j, :], in_=y_bank[:], func=ACT.Copy, scale=u1_column)
-                    else:
-                        nc.vector.tensor_scalar(
-                            out=y_t[:, j, :], in0=y_bank[:], scalar1=u1_column, scalar2=None, op0=ALU.mult
-                        )
-                y_scaled[(c, b)] = y_t
+                elif add_up:
+                    nc.vector.scalar_tensor_tensor(
+                        out=y_t[:, j, :],
+                        in0=y_bank[:],
+                        scalar=u1_column,
+                        in1=y_parts[c][0][:, j, :],
+                        op0=ALU.mult,
+                        op1=ALU.add,
+                    )
+                else:
+                    nc.scalar.activation(out=y_t[:, j, :], in_=y_bank[:], func=ACT.Copy, scale=u1_column)
+            y_parts[c] = [y_t] if add_up or b == 0 else y_parts[c] + [y_t]
 
         def store_out(c, engines=("scalar", "scalar")):
             if not in_range(c):
@@ -300,14 +308,14 @@ def tile_littlebititqspeclinear_pa_t_kernel(
                 for i in range(2):
                     columns_of_tile = slice((2 * half + i) * P, (2 * half + i + 1) * P)
                     for j in range(OUT_TILES):
-                        for b in range(BRANCHES):
+                        for part, y_t in enumerate(y_parts[c]):
                             nc.tensor.matmul(
                                 out=out_bank[:, i, j * P : (j + 1) * P],
-                                lhsT=y_scaled[(c, b)][:, j, columns_of_tile],
+                                lhsT=y_t[:, j, columns_of_tile],
                                 rhs=ident_f32[:],
                                 is_transpose=True,
-                                start=(b == 0),
-                                stop=(b == BRANCHES - 1),
+                                start=(part == 0),
+                                stop=(part == len(y_parts[c]) - 1),
                             )
                 if engines[half] == "scalar":
                     nc.scalar.copy(out=out_tile[:, 2 * half : 2 * half + 2, :], in_=out_bank[:])
@@ -415,34 +423,36 @@ def tile_littlebititqspeclinear_pa_t_kernel(
             if c == 0:
                 for b in range(BRANCHES):
                     quantise_u(b)
-            for b in range(BRANCHES):
-                quantise_x(c + 2, b)
+            quantise_x(c + 2, 0)
             group_h(c, 1, "vector", on_gpsimd)
+            quantise_x(c + 2, 1)
             quantise_h(c, 1)
             quantise_h(c, 0)
-            second_product(c - 1)
             first_product(c + 1, 0)
-            store_out(c - 1)
-            first_product(c + 1, 1, (0, 1))
+            for b in range(BRANCHES):
+                second_product(c - 1, b)
             transpose_x(c + 3)
-            first_product(c + 1, 1, (2, 3))
+            first_product(c + 1, 1, (0, 1))
+            first_product(c + 1, 1, (2, 3), "scalar" if c < N_CHUNKS - 3 else "vector")
+            store_out(c - 1)
 
         c = N_CHUNKS - 2
-        second_product(c - 1, (0,))
         group_h(c, 0, "vector")
-        second_product(c - 1, (1,), "vector")
+        second_product(c - 1, 0)
+        second_product(c - 1, 1, add_up=True)
         first_product(c + 1, 0)
         group_h(c, 1, "vector")
-        quantise_h(c, 1)
-        quantise_h(c, 0)
-        store_out(c - 1, ("vector", "vector"))
         first_product(c + 1, 1)
+        quantise_h(c, 0)
+        quantise_h(c, 1)
+        store_out(c - 1)
+        second_product(c, 0)
         for b in range(BRANCHES):
             group_h(c + 1, b, "vector")
         for b in range(BRANCHES):
             quantise_h(c + 1, b)
-        second_product(c)
-        second_product(c + 1, (0,))
-        second_product(c + 1, (1,), "vector")
+        second_product(c, 1, add_up=True)
+        second_product(c + 1, 0)
+        second_product(c + 1, 1, add_up=True)
         store_out(c, ("scalar", "vector"))
         store_out(c + 1, ("vector",))

@@ -68,15 +68,14 @@ def tile_littlebititqspeclinear_pa_t_kernel(
             x_tile = x_pool.tile([P, WIDTHS[c] // P, IN_F], BF16)
             source = rows_of(x_rows, c)
             n_loads = 2 if c == 1 else 1
+            n_tiles = WIDTHS[c] // P // n_loads
+            n_features = IN_F // 2 if c == 0 else IN_F
             for half in range(n_loads):
-                n_tiles = WIDTHS[c] // P // n_loads
                 tiles = slice(half * n_tiles, (half + 1) * n_tiles)
-                nc.sync.dma_start(out=x_tile[:, tiles, :], in_=source[:, tiles, :])
+                for first in range(0, IN_F, n_features):
+                    features = slice(first, first + n_features)
+                    nc.sync.dma_start(out=x_tile[:, tiles, features], in_=source[:, tiles, features])
             x_in[c] = x_tile
-
-        table_probe = const.tile([P, 1], F32)
-        nc.vector.memset(table_probe[:], 0.0)
-        nc.scalar.activation(out=table_probe[:], in_=table_probe[:], func=ACT.Sign)
 
         v2_rows = const.tile([P, PAIR * P], BF16)
         nc.gpsimd.memset(v2_rows[:], 0.0)
@@ -84,6 +83,12 @@ def tile_littlebititqspeclinear_pa_t_kernel(
             nc.sync.dma_start(
                 out=v2_rows[4 * b : 4 * b + 4, :], in_=vector.rearrange("o (f w) -> (o f) w", w=PAIR * P)
             )
+        load_x(0)
+
+        table_probe = const.tile([P, 1], F32)
+        nc.vector.memset(table_probe[:], 0.0)
+        nc.scalar.activation(out=table_probe[:], in_=table_probe[:], func=ACT.Sign)
+
         vector_rows = const.tile([P, P], BF16)
         nc.gpsimd.memset(vector_rows[:], 0.0)
         first_row = 0
@@ -112,7 +117,6 @@ def tile_littlebititqspeclinear_pa_t_kernel(
                 nc.sync.dma_start(out=v_tile[:, tiles, :], in_=source[:, tiles, :])
             v_in.append(v_tile)
 
-        load_x(0)
         load_v(V)
         load_x(1)
         load_v(V_R)
@@ -385,24 +389,23 @@ def tile_littlebititqspeclinear_pa_t_kernel(
 
         transpose_x(0)
         scale_x(0)
-        sign_v(0, (0,))
+        sign_v(0)
+        quantise_x(0, 0)
+        quantise_x(0, 1)
+        transpose_x(1)
 
         vector_bank = psum.tile([P, P], BF16, tag="bank")
         nc.tensor.transpose(vector_bank[:], vector_rows[:], ident_bf16[:])
         columns = const.tile([P, N_COLUMNS], F32)
-        nc.vector.tensor_copy(out=columns[:], in_=vector_bank[:, 0:N_COLUMNS])
         hidden_scale = const.tile([P, BRANCHES, HID_TILES], F32)
         v1_and_u2 = columns[:, V1_COL[0] : V1_COL[1] + 2 * HID_TILES].rearrange(
             "p (b v t) -> p b v t", b=BRANCHES, v=2
         )
 
-        sign_v(0, (1,))
-        quantise_x(0, 0)
-        nc.vector.tensor_tensor(out=hidden_scale[:], in0=v1_and_u2[:, :, 0, :], in1=v1_and_u2[:, :, 1, :], op=ALU.mult)
-        quantise_x(0, 1)
-        transpose_x(1)
         scale_x(1, (0,))
+        nc.vector.tensor_copy(out=columns[:], in_=vector_bank[:, 0:N_COLUMNS])
         quantise_v(0)
+        nc.vector.tensor_tensor(out=hidden_scale[:], in0=v1_and_u2[:, :, 0, :], in1=v1_and_u2[:, :, 1, :], op=ALU.mult)
         scale_x(1, (1,))
         sign_v(1)
         first_product(0, 0)
@@ -429,10 +432,11 @@ def tile_littlebititqspeclinear_pa_t_kernel(
             quantise_h(c, 1)
             quantise_h(c, 0)
             first_product(c + 1, 0)
+            first_product(c + 1, 1, (0,))
             for b in range(BRANCHES):
                 second_product(c - 1, b)
             transpose_x(c + 3)
-            first_product(c + 1, 1, (0, 1))
+            first_product(c + 1, 1, (1,))
             first_product(c + 1, 1, (2, 3), "scalar" if c < N_CHUNKS - 3 else "vector")
             store_out(c - 1)
 

@@ -163,7 +163,7 @@ def tile_littlebititqspeclinear_pa_t_kernel(
                 columns_of_half = slice(half * HALF, (half + 1) * HALF)
                 for b in range(BRANCHES):
                     if (c, b) not in x_scaled:
-                        scaled = one_chunk.tile([P, X_PASSES, WIDTHS[c], PACK], BF16, align_bytes=64)
+                        scaled = one_chunk.tile([P, X_PASSES, WIDTHS[c], PACK], BF16, align_bytes=256)
                         x_scaled[(c, b)] = scaled
                     nc.vector.tensor_tensor(
                         out=x_scaled[(c, b)][:, g, columns_of_half, :].rearrange("p c (u e) -> p c u e", e=PAIR),
@@ -180,8 +180,8 @@ def tile_littlebititqspeclinear_pa_t_kernel(
         def quantise_x(c, b):
             if not in_range(c):
                 return
-            x_codes = two_chunks.tile([P, X_PASSES, WIDTHS[c]], U32, align_bytes=64)
-            x_scales = two_chunks.tile([P, X_PASSES, WIDTHS[c]], U8, align_bytes=64)
+            x_codes = two_chunks.tile([P, X_PASSES, WIDTHS[c]], U32, align_bytes=256)
+            x_scales = two_chunks.tile([P, X_PASSES, WIDTHS[c]], U8, align_bytes=256)
             nc.vector.quantize_mx(
                 out=x_codes[:].rearrange("p g c -> p (g c)").bitcast(FP8X4),
                 scales=x_scales[:].rearrange("p g c -> p (g c)"),
@@ -228,7 +228,7 @@ def tile_littlebititqspeclinear_pa_t_kernel(
             if not in_range(c):
                 return
             if (c, b) not in h_grouped:
-                grouped = one_chunk.tile([P, WIDTHS[c], PACK], BF16, align_bytes=64)
+                grouped = one_chunk.tile([P, WIDTHS[c], PACK], BF16, align_bytes=256)
                 h_grouped[(c, b)] = grouped
             grouped = h_grouped[(c, b)]
             columns_here = slice(first, min(last, WIDTHS[c]))
@@ -252,8 +252,8 @@ def tile_littlebititqspeclinear_pa_t_kernel(
         def quantise_h(c, b):
             if not in_range(c):
                 return
-            h_codes = two_chunks.tile([P, WIDTHS[c]], U32, align_bytes=64)
-            h_scales = two_chunks.tile([P, WIDTHS[c]], U8, align_bytes=64)
+            h_codes = two_chunks.tile([P, WIDTHS[c]], U32, align_bytes=256)
+            h_scales = two_chunks.tile([P, WIDTHS[c]], U8, align_bytes=256)
             nc.vector.quantize_mx(
                 out=h_codes[:].bitcast(FP8X4),
                 scales=h_scales[:],
@@ -332,7 +332,7 @@ def tile_littlebititqspeclinear_pa_t_kernel(
         def sign_v(b, halves=(0, 1)):
             v_words = v_in[b][:].bitcast(F32)
             if b not in v_signs_of:
-                v_signs = weight_stage.tile([P, X_PASSES, HID_F, PACK], BF16, align_bytes=64)
+                v_signs = weight_stage.tile([P, X_PASSES, HID_F, PACK], BF16, align_bytes=256)
                 v_signs_of[b] = v_signs
             v_signs = v_signs_of[b]
             for half in halves:
@@ -353,8 +353,8 @@ def tile_littlebititqspeclinear_pa_t_kernel(
                     )
 
         def quantise_v(b):
-            v_codes = const.tile([P, X_PASSES, HID_F], U32, align_bytes=64, name="v_codes%d" % b)
-            v_scales = const.tile([P, X_PASSES, HID_F], U8, align_bytes=64, name="v_scales%d" % b)
+            v_codes = const.tile([P, X_PASSES, HID_F], U32, align_bytes=256, name="v_codes%d" % b)
+            v_scales = const.tile([P, X_PASSES, HID_F], U8, align_bytes=256, name="v_scales%d" % b)
             nc.vector.quantize_mx(
                 out=v_codes[:].rearrange("p g s -> p (g s)").bitcast(FP8X4),
                 scales=v_scales[:].rearrange("p g s -> p (g s)"),
@@ -371,13 +371,13 @@ def tile_littlebititqspeclinear_pa_t_kernel(
                     nc.tensor.transpose(
                         u_bank[:, t, j * P : (j + 1) * P], u_in[b][:, j, t * P : (t + 1) * P], ident_bf16[:]
                     )
-            u_signs = weight_stage.tile([P, OUT_F, PACK], BF16, align_bytes=64)
+            u_signs = weight_stage.tile([P, OUT_F, PACK], BF16, align_bytes=256)
             nc.scalar.activation(out=u_signs[:], in_=u_bank[:].rearrange("p t o -> p o t"), func=ACT.Sign)
             u_signs_of[b] = u_signs
 
         def quantise_u(b):
-            u_codes = const.tile([P, OUT_F], U32, align_bytes=64, name="u_codes%d" % b)
-            u_scales = const.tile([P, OUT_F], U8, align_bytes=64, name="u_scales%d" % b)
+            u_codes = const.tile([P, OUT_F], U32, align_bytes=256, name="u_codes%d" % b)
+            u_scales = const.tile([P, OUT_F], U8, align_bytes=256, name="u_scales%d" % b)
             nc.vector.quantize_mx(
                 out=u_codes[:].bitcast(FP8X4), scales=u_scales[:], in_=u_signs_of[b][:].rearrange("p o t -> p (o t)")
             )

@@ -79,11 +79,11 @@ def tile_littlebititqspeclinear_pa_t_kernel(
 
         v2_rows = const.tile([P, PAIR * P], BF16)
         nc.gpsimd.memset(v2_rows[:], 0.0)
+        load_x(0)
         for b, vector in enumerate((v2, v2_R)):
             nc.sync.dma_start(
                 out=v2_rows[4 * b : 4 * b + 4, :], in_=vector.rearrange("o (f w) -> (o f) w", w=PAIR * P)
             )
-        load_x(0)
 
         table_probe = const.tile([P, 1], F32)
         nc.vector.memset(table_probe[:], 0.0)
@@ -136,13 +136,13 @@ def tile_littlebititqspeclinear_pa_t_kernel(
 
         x_banks = {}
 
-        def transpose_x(c):
+        def transpose_x(c, passes=range(X_PASSES)):
             if not in_range(c):
                 return
             x_words = x_in[c][:].bitcast(F32)
-            x_banks[c] = []
+            x_banks.setdefault(c, [])
             for half in range(WIDTHS[c] // HALF):
-                for g in range(X_PASSES):
+                for g in passes:
                     x_bank = x_psum.tile([P, 2, HALF], F32)
                     for u in range(2):
                         words = slice((2 * g + u) * P, (2 * g + u + 1) * P)
@@ -383,11 +383,12 @@ def tile_littlebititqspeclinear_pa_t_kernel(
             )
             u_mx.append((u_codes, u_scales))
 
+        transpose_x(0, (0,))
         v2_bank = psum.tile([P, P], F32, tag="bank")
         nc.tensor.transpose(v2_bank[:], v2_rows[:].bitcast(F32), ident_f32[:])
         nc.vector.tensor_copy(out=v2_words[:], in_=v2_bank[:, 0 : BRANCHES * X_PASSES * 2])
 
-        transpose_x(0)
+        transpose_x(0, (1,))
         scale_x(0)
         sign_v(0)
         quantise_x(0, 0)

@@ -242,10 +242,12 @@ def tile_littlebititqspeclinear_pa_t_kernel(
                     op1=ALU.add,
                 )
             else:
-                nc.vector.tensor_copy(
-                    out=grouped[:, columns_here, :].rearrange("p (c i) t -> p c t i", i=4),
-                    in_=h_planes[(c, b)][:, :, columns_here].rearrange("p t (c i) -> p c t i", i=4),
-                )
+                runs_out = grouped[:, columns_here, :].rearrange("p (c i) t -> p c t i", i=4)
+                runs_in = h_planes[(c, b)][:, :, columns_here].rearrange("p t (c i) -> p c t i", i=4)
+                if engine == "scalar":
+                    nc.scalar.copy(out=runs_out, in_=runs_in)
+                else:
+                    nc.vector.tensor_copy(out=runs_out, in_=runs_in)
 
         h_mx = {}
 
@@ -428,14 +430,17 @@ def tile_littlebititqspeclinear_pa_t_kernel(
                 for b in range(BRANCHES):
                     quantise_u(b)
             quantise_x(c + 2, 0)
-            group_h(c, 1, "vector", on_gpsimd)
-            quantise_x(c + 2, 1)
-            quantise_h(c, 1)
-            quantise_h(c, 0)
             first_product(c + 1, 0)
             first_product(c + 1, 1, (0,))
             for b in range(BRANCHES):
                 second_product(c - 1, b)
+            on_scalar = P if WIDTHS[c] == CHUNK and c < N_CHUNKS // 2 else 0
+            group_h(c, 1, "vector", on_gpsimd, WIDTHS[c] - on_scalar)
+            if on_scalar > 0:
+                group_h(c, 1, "scalar", WIDTHS[c] - on_scalar)
+            quantise_x(c + 2, 1)
+            quantise_h(c, 1)
+            quantise_h(c, 0)
             transpose_x(c + 3)
             first_product(c + 1, 1, (1,))
             first_product(c + 1, 1, (2, 3), "scalar" if c < N_CHUNKS - 3 else "vector")

from contextlib import ExitStack

import concourse.mybir as mybir
from concourse.masks import make_identity

F32 = mybir.dt.float32
BF16 = mybir.dt.bfloat16
U32 = mybir.dt.uint32
U8 = mybir.dt.uint8
FP8X4 = mybir.dt.float8_e4m3fn_x4
ACT = mybir.ActivationFunctionType
ALU = mybir.AluOpType

P = 128
PACK = 4
PAIR = 2
K_PASS = P * PACK

ROWS = 4096
IN_F = 1024
HID_F = 512
OUT_F = 256
BRANCHES = 2

CHUNK = 512
HALF = 256
WIDTHS = [HALF] + [CHUNK] * (ROWS // CHUNK - 1) + [HALF]
FIRST_ROWS = [sum(WIDTHS[:c]) for c in range(len(WIDTHS))]
N_CHUNKS = len(WIDTHS)
X_PASSES = IN_F // K_PASS
HID_TILES = HID_F // P
OUT_TILES = OUT_F // P
assert HID_F == K_PASS and HID_TILES == PACK

V1_COL = (0, 8)
U1_COL = (16, 18)
BIAS_COL = 20
N_COLUMNS = 22

FLOPS = BRANCHES * 2 * ROWS * (IN_F * HID_F + HID_F * OUT_F)


def tile_littlebititqspeclinear_pa_t_kernel(
    tc, x, V, U, v2, v1, u2, u1, V_R, U_R, v2_R, v1_R, u2_R, u1_R, bias, out
):
    nc = tc.nc
    x_rows = x.flatten_outer_dims()
    out_rows = out.flatten_outer_dims()

    with ExitStack() as pools:
        pools.enter_context(tc.manual_schedule())
        const = pools.enter_context(tc.tile_pool(name="const", bufs=1))
        weight_stage = pools.enter_context(tc.tile_pool(name="weight_stage", bufs=2))
        x_pool = pools.enter_context(tc.tile_pool(name="x_pool", bufs=8))
        one_chunk = pools.enter_context(tc.tile_pool(name="one_chunk", bufs=BRANCHES))
        two_chunks = pools.enter_context(tc.tile_pool(name="two_chunks", bufs=2 * BRANCHES))
        out_pool = pools.enter_context(tc.tile_pool(name="out_pool", bufs=2))
        x_psum = pools.enter_context(tc.psum_pool(name="x_psum", bufs=4))
        psum = pools.enter_context(tc.psum_pool(name="psum", bufs=4))

        x_in = {}

        def rows_of(dram, c):
            chunk = dram[FIRST_ROWS[c] : FIRST_ROWS[c] + WIDTHS[c], :]
            return chunk.rearrange("(p i) k -> p i k", i=WIDTHS[c] // P)

        def load_x(c):
            x_tile = x_pool.tile([P, WIDTHS[c] // P, IN_F], BF16)
            source = rows_of(x_rows, c)
            n_loads = 2 if c == 1 else 1
            n_tiles = WIDTHS[c] // P // n_loads
            n_features = IN_F // 2 if c == 0 else IN_F
            for half in range(n_loads):
                tiles = slice(half * n_tiles, (half + 1) * n_tiles)
                for first in range(0, IN_F, n_features):
                    features = slice(first, first + n_features)
                    nc.sync.dma_start(out=x_tile[:, tiles, features], in_=source[:, tiles, features])
            x_in[c] = x_tile

        v2_rows = const.tile([P, PAIR * P], BF16)
        nc.gpsimd.memset(v2_rows[:], 0.0)
        load_x(0)
        for b, vector in enumerate((v2, v2_R)):
            nc.sync.dma_start(
                out=v2_rows[4 * b : 4 * b + 4, :], in_=vector.rearrange("o (f w) -> (o f) w", w=PAIR * P)
            )

        table_probe = const.tile([P, 1], F32)
        nc.vector.memset(table_probe[:], 0.0)
        nc.scalar.activation(out=table_probe[:], in_=table_probe[:], func=ACT.Sign)

        vector_rows = const.tile([P, P], BF16)
        nc.gpsimd.memset(vector_rows[:], 0.0)
        first_row = 0
        for vector in (v1, u2, v1_R, u2_R, u1, u1_R):
            n_rows = vector.shape[1] // P
            nc.scalar.dma_start(
                out=vector_rows[first_row : first_row + n_rows, :], in_=vector.rearrange("o (j p) -> (o j) p", p=P)
            )
            first_row += n_rows
        nc.scalar.dma_start(
            out=vector_rows[BIAS_COL : BIAS_COL + OUT_TILES, :], in_=bias.rearrange("(j p) -> j p", p=P)
        )

        ident_f32 = const.tile([P, P], F32)
        make_identity(nc, ident_f32[:])
        ident_bf16 = const.tile([P, P], BF16)
        make_identity(nc, ident_bf16[:])

        v_in = []

        def load_v(weight):
            v_tile = weight_stage.tile([P, HID_TILES, IN_F], BF16)
            source = weight.rearrange("(m p) k -> p m k", p=P)
            for half in range(2):
                tiles = slice(half * 2, half * 2 + 2)
                nc.sync.dma_start(out=v_tile[:, tiles, :], in_=source[:, tiles, :])
            v_in.append(v_tile)

        load_v(V)
        load_x(1)
        load_v(V_R)
        u_in = []
        for weight in (U, U_R):
            u_tile = weight_stage.tile([P, OUT_TILES, HID_F], BF16)
            nc.sync.dma_start(out=u_tile[:], in_=weight.rearrange("(j p) s -> p j s", p=P))
            u_in.append(u_tile)
        for c in range(2, N_CHUNKS):
            load_x(c)

        def in_range(c):
            return 0 <= c < N_CHUNKS

        v2_words = const.tile([P, BRANCHES * X_PASSES * 2], F32)
        v2_values = v2_words[:].bitcast(BF16).rearrange("p (b g t) -> p b g t", b=BRANCHES, g=X_PASSES)

        x_banks = {}

        def transpose_x(c, passes=range(X_PASSES)):
            if not in_range(c):
                return
            x_words = x_in[c][:].bitcast(F32)
            x_banks.setdefault(c, [])
            for half in range(WIDTHS[c] // HALF):
                for g in passes:
                    x_bank = x_psum.tile([P, 2, HALF], F32)
                    for u in range(2):
                        words = slice((2 * g + u) * P, (2 * g + u + 1) * P)
                        for i in range(2):
                            nc.tensor.transpose(
                                x_bank[:, u, i * P : (i + 1) * P], x_words[:, 2 * half + i, words], ident_f32[:]
                            )
                    x_banks[c].append((half, g, x_bank))

        x_scaled = {}

        def scale_x(c, halves=(0, 1)):
            if not in_range(c):
                return
            for half, g, x_bank in x_banks[c]:
                if half not in halves:
                    continue
                columns_of_half = slice(half * HALF, (half + 1) * HALF)
                for b in range(BRANCHES):
                    if (c, b) not in x_scaled:
                        scaled = one_chunk.tile([P, X_PASSES, WIDTHS[c], PACK], BF16, align_bytes=256)
                        x_scaled[(c, b)] = scaled
                    nc.vector.tensor_tensor(
                        out=x_scaled[(c, b)][:, g, columns_of_half, :].rearrange("p c (u e) -> p c u e", e=PAIR),
                        in0=x_bank[:].bitcast(BF16).rearrange("p u (c e) -> p c u e", e=PAIR),
                        in1=v2_values[:, b, g, :]
                        .rearrange("p (u e) -> p u e", e=PAIR)
                        .unsqueeze(1)
                        .to_broadcast([P, HALF, 2, PAIR]),
                        op=ALU.mult,
                    )

        x_mx = {}

        def quantise_x(c, b):
            if not in_range(c):
                return
            x_codes = two_chunks.tile([P, X_PASSES, WIDTHS[c]], U32, align_bytes=256)
            x_scales = two_chunks.tile([P, X_PASSES, WIDTHS[c]], U8, align_bytes=256)
            nc.vector.quantize_mx(
                out=x_codes[:].rearrange("p g c -> p (g c)").bitcast(FP8X4),
                scales=x_scales[:].rearrange("p g c -> p (g c)"),
                in_=x_scaled[(c, b)][:].rearrange("p g c t -> p (g c t)"),
            )
            x_mx[(c, b)] = (x_codes, x_scales)

        v_mx = []
        u_mx = []
        h_planes = {}

        def first_product(c, b, tiles=range(HID_TILES), engine="scalar"):
            if in_range(c):
                v_codes, v_scales = v_mx[b]
                x_codes, x_scales = x_mx[(c, b)]
                if (c, b) not in h_planes:
                    h_plane = two_chunks.tile([P, HID_TILES, WIDTHS[c]], BF16)
                    h_planes[(c, b)] = h_plane
                h_plane = h_planes[(c, b)]
                for t in tiles:
                    features = slice(t * P, (t + 1) * P)
                    h_bank = psum.tile([P, WIDTHS[c]], F32, tag="bank")
                    for g in range(X_PASSES):
                        nc.tensor.matmul_mx(
                            out=h_bank[:],
                            lhsT=v_codes[:, g, features].bitcast(FP8X4),
                            lhsT_scale=v_scales[:, g, features],
                            rhs=x_codes[:, g, :].bitcast(FP8X4),
                            rhs_scale=x_scales[:, g, :],
                            start=(g == 0),
                            stop=(g == X_PASSES - 1),
                        )
                    scale_column = hidden_scale[:, b, t : t + 1]
                    if engine == "scalar":
                        nc.scalar.activation(out=h_plane[:, t, :], in_=h_bank[:], func=ACT.Copy, scale=scale_column)
                    else:
                        nc.vector.tensor_scalar(
                            out=h_plane[:, t, :], in0=h_bank[:], scalar1=scale_column, scalar2=None, op0=ALU.mult
                        )

        h_grouped = {}

        def group_h(c, b, engine, first=0, last=CHUNK):
            if not in_range(c):
                return
            if (c, b) not in h_grouped:
                grouped = one_chunk.tile([P, WIDTHS[c], PACK], BF16, align_bytes=256)
                h_grouped[(c, b)] = grouped
            grouped = h_grouped[(c, b)]
            columns_here = slice(first, min(last, WIDTHS[c]))
            if engine == "gpsimd":
                nc.gpsimd.tensor_scalar(
                    out=grouped[:, columns_here, :],
                    in0=h_planes[(c, b)][:, :, columns_here].rearrange("p t c -> p c t"),
                    scalar1=1.0,
                    scalar2=0.0,
                    op0=ALU.mult,
                    op1=ALU.add,
                )
            else:
                runs_out = grouped[:, columns_here, :].rearrange("p (c i) t -> p c t i", i=4)
                runs_in = h_planes[(c, b)][:, :, columns_here].rearrange("p t (c i) -> p c t i", i=4)
                if engine == "scalar":
                    nc.scalar.copy(out=runs_out, in_=runs_in)
                else:
                    nc.vector.tensor_copy(out=runs_out, in_=runs_in)

        h_mx = {}

        def quantise_h(c, b):
            if not in_range(c):
                return
            h_codes = two_chunks.tile([P, WIDTHS[c]], U32, align_bytes=256)
            h_scales = two_chunks.tile([P, WIDTHS[c]], U8, align_bytes=256)
            nc.vector.quantize_mx(
                out=h_codes[:].bitcast(FP8X4),
                scales=h_scales[:],
                in_=h_grouped[(c, b)][:].rearrange("p c t -> p (c t)"),
            )
            h_mx[(c, b)] = (h_codes, h_scales)

        y_parts = {}

        def second_product(c, b, add_up=False):
            if not in_range(c):
                return
            u_codes, u_scales = u_mx[b]
            h_codes, h_scales = h_mx[(c, b)]
            y_t = two_chunks.tile([P, OUT_TILES, WIDTHS[c]], F32)
            for j in range(OUT_TILES):
                features = slice(j * P, (j + 1) * P)
                y_bank = psum.tile([P, WIDTHS[c]], F32, tag="bank")
                nc.tensor.matmul_mx(
                    out=y_bank[:],
                    lhsT=u_codes[:, features].bitcast(FP8X4),
                    lhsT_scale=u_scales[:, features],
                    rhs=h_codes[:].bitcast(FP8X4),
                    rhs_scale=h_scales[:],
                    start=True,
                    stop=True,
                )
                u1_column = columns[:, U1_COL[b] + j : U1_COL[b] + j + 1]
                if b == 0:
                    nc.scalar.activation(
                        out=y_t[:, j, :],
                        in_=y_bank[:],
                        func=ACT.Identity,
                        scale=u1_column,
                        bias=columns[:, BIAS_COL + j : BIAS_COL + j + 1],
                    )
                elif add_up:
                    nc.vector.scalar_tensor_tensor(
                        out=y_t[:, j, :],
                        in0=y_bank[:],
                        scalar=u1_column,
                        in1=y_parts[c][0][:, j, :],
                        op0=ALU.mult,
                        op1=ALU.add,
                    )
                else:
                    nc.scalar.activation(out=y_t[:, j, :], in_=y_bank[:], func=ACT.Copy, scale=u1_column)
            y_parts[c] = [y_t] if add_up or b == 0 else y_parts[c] + [y_t]

        def store_out(c, engines=("scalar", "scalar")):
            if not in_range(c):
                return
            out_tile = out_pool.tile([P, WIDTHS[c] // P, OUT_F], F32)
            for half in range(WIDTHS[c] // HALF):
                out_bank = psum.tile([P, 2, OUT_F], F32, tag="bank")
                for i in range(2):
                    columns_of_tile = slice((2 * half + i) * P, (2 * half + i + 1) * P)
                    for j in range(OUT_TILES):
                        for part, y_t in enumerate(y_parts[c]):
                            nc.tensor.matmul(
                                out=out_bank[:, i, j * P : (j + 1) * P],
                                lhsT=y_t[:, j, columns_of_tile],
                                rhs=ident_f32[:],
                                is_transpose=True,
                                start=(part == 0),
                                stop=(part == len(y_parts[c]) - 1),
                            )
                if engines[half] == "scalar":
                    nc.scalar.copy(out=out_tile[:, 2 * half : 2 * half + 2, :], in_=out_bank[:])
                else:
                    nc.vector.tensor_copy(out=out_tile[:, 2 * half : 2 * half + 2, :], in_=out_bank[:])
            nc.sync.dma_start(out=rows_of(out_rows, c), in_=out_tile[:])

        v_signs_of = {}

        def sign_v(b, halves=(0, 1)):
            v_words = v_in[b][:].bitcast(F32)
            if b not in v_signs_of:
                v_signs = weight_stage.tile([P, X_PASSES, HID_F, PACK], BF16, align_bytes=256)
                v_signs_of[b] = v_signs
            v_signs = v_signs_of[b]
            for half in halves:
                for g in range(X_PASSES):
                    v_bank = psum.tile([P, 2, HALF], F32, tag="bank")
                    for u in range(2):
                        words = slice((2 * g + u) * P, (2 * g + u + 1) * P)
                        for i in range(2):
                            nc.tensor.transpose(
                                v_bank[:, u, i * P : (i + 1) * P], v_words[:, 2 * half + i, words], ident_f32[:]
                            )
                    nc.scalar.activation(
                        out=v_signs[:, g, half * HALF : (half + 1) * HALF, :].rearrange(
                            "p c (u e) -> p c u e", e=PAIR
                        ),
                        in_=v_bank[:].bitcast(BF16).rearrange("p u (c e) -> p c u e", e=PAIR),
                        func=ACT.Sign,
                    )

        def quantise_v(b):
            v_codes = const.tile([P, X_PASSES, HID_F], U32, align_bytes=256, name="v_codes%d" % b)
            v_scales = const.tile([P, X_PASSES, HID_F], U8, align_bytes=256, name="v_scales%d" % b)
            nc.vector.quantize_mx(
                out=v_codes[:].rearrange("p g s -> p (g s)").bitcast(FP8X4),
                scales=v_scales[:].rearrange("p g s -> p (g s)"),
                in_=v_signs_of[b][:].rearrange("p g s t -> p (g s t)"),
            )
            v_mx.append((v_codes, v_scales))

        u_signs_of = {}

        def sign_u(b):
            u_bank = psum.tile([P, PACK, OUT_F], BF16, tag="bank")
            for t in range(PACK):
                for j in range(OUT_TILES):
                    nc.tensor.transpose(
                        u_bank[:, t, j * P : (j + 1) * P], u_in[b][:, j, t * P : (t + 1) * P], ident_bf16[:]
                    )
            u_signs = weight_stage.tile([P, OUT_F, PACK], BF16, align_bytes=256)
            nc.scalar.activation(out=u_signs[:], in_=u_bank[:].rearrange("p t o -> p o t"), func=ACT.Sign)
            u_signs_of[b] = u_signs

        def quantise_u(b):
            u_codes = const.tile([P, OUT_F], U32, align_bytes=256, name="u_codes%d" % b)
            u_scales = const.tile([P, OUT_F], U8, align_bytes=256, name="u_scales%d" % b)
            nc.vector.quantize_mx(
                out=u_codes[:].bitcast(FP8X4), scales=u_scales[:], in_=u_signs_of[b][:].rearrange("p o t -> p (o t)")
            )
            u_mx.append((u_codes, u_scales))

        transpose_x(0, (0,))
        v2_bank = psum.tile([P, P], F32, tag="bank")
        nc.tensor.transpose(v2_bank[:], v2_rows[:].bitcast(F32), ident_f32[:])
        nc.vector.tensor_copy(out=v2_words[:], in_=v2_bank[:, 0 : BRANCHES * X_PASSES * 2])

        transpose_x(0, (1,))
        scale_x(0)
        sign_v(0)
        quantise_x(0, 0)
        quantise_x(0, 1)
        transpose_x(1)

        vector_bank = psum.tile([P, P], BF16, tag="bank")
        nc.tensor.transpose(vector_bank[:], vector_rows[:], ident_bf16[:])
        columns = const.tile([P, N_COLUMNS], F32)
        hidden_scale = const.tile([P, BRANCHES, HID_TILES], F32)
        v1_and_u2 = columns[:, V1_COL[0] : V1_COL[1] + 2 * HID_TILES].rearrange(
            "p (b v t) -> p b v t", b=BRANCHES, v=2
        )

        scale_x(1, (0,))
        nc.vector.tensor_copy(out=columns[:], in_=vector_bank[:, 0:N_COLUMNS])
        quantise_v(0)
        nc.vector.tensor_tensor(out=hidden_scale[:], in0=v1_and_u2[:, :, 0, :], in1=v1_and_u2[:, :, 1, :], op=ALU.mult)
        scale_x(1, (1,))
        sign_v(1)
        first_product(0, 0)
        transpose_x(2)
        quantise_x(1, 0)
        quantise_v(1)
        quantise_x(1, 1)
        first_product(0, 1)
        for b in range(BRANCHES):
            sign_u(b)

        for c in range(N_CHUNKS - 2):
            group_h(c, 0, "gpsimd")
            on_gpsimd = WIDTHS[c] // 2 if WIDTHS[c + 2] == CHUNK else 0
            if on_gpsimd > 0:
                group_h(c, 1, "gpsimd", 0, on_gpsimd)
            scale_x(c + 2)
            if c == 0:
                for b in range(BRANCHES):
                    quantise_u(b)
            quantise_x(c + 2, 0)
            first_product(c + 1, 0)
            first_product(c + 1, 1, (0,))
            for b in range(BRANCHES):
                second_product(c - 1, b)
            on_scalar = P if WIDTHS[c] == CHUNK and c < N_CHUNKS // 2 else 0
            group_h(c, 1, "vector", on_gpsimd, WIDTHS[c] - on_scalar)
            if on_scalar > 0:
                group_h(c, 1, "scalar", WIDTHS[c] - on_scalar)
            quantise_x(c + 2, 1)
            quantise_h(c, 1)
            quantise_h(c, 0)
            transpose_x(c + 3)
            first_product(c + 1, 1, (1,))
            first_product(c + 1, 1, (2, 3), "scalar" if c < N_CHUNKS - 3 else "vector")
            store_out(c - 1)

        c = N_CHUNKS - 2
        group_h(c, 0, "vector")
        second_product(c - 1, 0)
        second_product(c - 1, 1, add_up=True)
        first_product(c + 1, 0)
        group_h(c, 1, "vector")
        first_product(c + 1, 1)
        quantise_h(c, 0)
        quantise_h(c, 1)
        store_out(c - 1)
        second_product(c, 0)
        for b in range(BRANCHES):
            group_h(c + 1, b, "vector")
        for b in range(BRANCHES):
            quantise_h(c + 1, b)
        second_product(c, 1, add_up=True)
        second_product(c + 1, 0)
        second_product(c + 1, 1, add_up=True)
        store_out(c, ("scalar", "vector"))
        store_out(c + 1, ("vector",))
